import numpy as np
import ml_dtypes


def mxq(x, axis, fmt="e4m3"):
    dtype, down = {"e4m3": (ml_dtypes.float8_e4m3fn, 7), "e5m2": (ml_dtypes.float8_e5m2, 14)}[fmt]
    v = np.moveaxis(np.asarray(x, np.float32).astype(ml_dtypes.bfloat16).astype(np.float64), axis, -1)
    blocks = v.reshape(v.shape[:-1] + (-1, 32))
    amax = np.abs(blocks).max(-1, keepdims=True)
    byte = np.maximum(np.where(amax > 0, np.frexp(amax)[1] - 1 + 127, 0) - down, 1)
    scale = np.exp2(byte - 127.0)
    codes = (blocks / scale).astype(np.float32).astype(dtype).astype(np.float64)
    return np.moveaxis((codes * scale).reshape(v.shape), -1, axis)


WIDE = False


def mx_kscale(k):
    if not WIDE:
        return np.ones(k)
    levels = np.array([30, -30])
    if k % 512:
        return np.exp2(np.random.permutation(np.resize(levels, k // 32))).repeat(32)
    a = np.empty((k // 512, 16))
    for p in range(k // 512):
        a[p, :8] = np.random.permutation(np.resize(levels, 8))
        for g in range(8):
            far = levels[np.abs(levels - a[p, g]) >= 10]
            a[p, g + 8] = far[np.random.randint(len(far))]
    return np.exp2(a.ravel()).repeat(32)


BF16 = ml_dtypes.bfloat16


def bf(x):
    return np.asarray(x, np.float32).astype(BF16)


def f64(x):
    return np.asarray(x).astype(np.float64)


E2M1 = np.array([0.0, 0.5, 1.0, 1.5, 2.0, 3.0, 4.0, 6.0, -0.0, -0.5, -1.0, -1.5, -2.0, -3.0, -4.0, -6.0])


def pack_weight(w, fmt):
    k, n = w.shape
    w = f64(bf(w)).reshape(k // 32, 32, n)
    amax = np.abs(w).max(1)
    if fmt == "e4m3":
        byte = np.frexp(amax)[1] - 1 + 127 - 7
    else:
        mant, ex = np.frexp(amax / 6.0)
        byte = np.where(mant > 0.5, ex, ex - 1) + 127
    byte = np.clip(np.where(amax > 0, byte, 1), 1, 254)
    scaled = (w * np.exp2(127.0 - byte)[:, None, :]).reshape(k, n).astype(np.float32)
    by_word = np.ascontiguousarray(scaled.reshape(k // 512, 128, 4, n).transpose(0, 1, 3, 2))
    if fmt == "e4m3":
        words = by_word.astype(ml_dtypes.float8_e4m3fn).view(np.uint8)
    else:
        c = by_word.astype(ml_dtypes.float4_e2m1fn).view(np.uint8) & 0xF
        words = c[..., 0::2] | (c[..., 1::2] << 4)
    return np.ascontiguousarray(words), np.ascontiguousarray(byte.astype(np.uint8).reshape(k // 512, 16, n))


def unpack_weight(words, scales, fmt):
    g, p, n, _ = words.shape
    if fmt == "e4m3":
        vals = np.ascontiguousarray(words).view(ml_dtypes.float8_e4m3fn).astype(np.float64)
    else:
        nib = np.empty((g, p, n, 4), np.uint8)
        nib[..., 0::2] = words & 0xF
        nib[..., 1::2] = words >> 4
        vals = E2M1[nib]
    vals = vals * np.repeat(np.exp2(scales.astype(np.float64) - 127.0), 8, axis=1)[..., None]
    return vals.transpose(0, 1, 3, 2).reshape(g * 512, n)

def pack4(w):
    words, scales = pack_weight(w, "e2m1")
    return words.reshape(words.shape[0], 128, -1), scales


def unpack4(words, scales):
    return unpack_weight(words.reshape(words.shape[0], 128, -1, 2), scales, "e2m1")


B, S, C, HD = 1, 512, 3072, 128
H = C // HD
HP = HD // 2
EPS = 1e-6
THETA = 10000.0


def rmsnorm(h, g):
    return h * (1.0 / np.sqrt(np.mean(h * h, axis=-1, keepdims=True) + EPS)) * g


def apply_rope1(h, freqs):
    sh = h.shape
    h_ = h.reshape(*sh[:-1], -1, 1, 2)
    out = freqs[..., 0] * h_[..., 0] + freqs[..., 1] * h_[..., 1]
    return out.reshape(sh)


def setup_inputs():
    s = mx_kscale(C)
    pos = f64(np.random.randint(0, S, size=(S, 1)))
    inv_freq = 1.0 / THETA ** (np.arange(HP) / HP)
    ang = pos * inv_freq
    cos, sin = np.cos(ang), np.sin(ang)
    rot = np.stack([np.stack([cos, -sin], -1), np.stack([sin, cos], -1)], -2)
    x = bf(np.random.standard_normal((B, S, C)) * s)
    w = np.random.standard_normal((C, C)) / np.sqrt(C) / s[None, :]
    w_words, w_scales = pack4(np.ascontiguousarray(w.T))
    return {"x": x,
            "freqs": bf(rot[None, :, None]),
            "w_words": w_words,
            "w_scales": w_scales,
            "b": bf(np.random.standard_normal(C) * 0.3),
            "g": bf(1.0 + 0.1 * np.random.standard_normal(HD))}


def reference(x, freqs, w_words, w_scales, b, g):
    p = (mxq(f64(x), 2, "e5m2") @ unpack4(w_words, w_scales)) + f64(b)
    h = p.reshape(B, S, H, HD)
    return apply_rope1(rmsnorm(h, f64(g)), f64(freqs))

@@ -1,0 +1,302 @@
+from contextlib import ExitStack
+
+import concourse.mybir as mybir
+from concourse.masks import make_identity
+
+S, C, HD = 512, 3072, 128
+EPS = 1e-6
+FLOPS = 2 * S * C * C
+
+F32 = mybir.dt.float32
+BF16 = mybir.dt.bfloat16
+I32 = mybir.dt.int32
+U32 = mybir.dt.uint32
+U8 = mybir.dt.uint8
+E5M2 = mybir.dt.float8_e5m2_x4
+E2M1 = mybir.dt.float4_e2m1fn_x4
+ALU = mybir.AluOpType
+ACT = mybir.ActivationFunctionType
+
+P = 128
+PASSES = C // 512
+TILES = S // P
+NCOL = 512
+CHUNKS = C // NCOL
+HEADS = NCOL // HD
+THIRDS = PASSES // 2
+LOADS = ((0, 1), (1, 2), (2, 3), (3, 6))
+ORDER = (
+    [(t, c) for c in range(3) for t in range(2)]
+    + [(2, c) for c in range(3)]
+    + [(t, c) for c in range(3, 5) for t in range(3)]
+    + [(3, c) for c in range(5)]
+    + [(t, 5) for t in range(4)]
+)
+
+
+def tile_selfattention_pa_kernel(tc, x, freqs, w_words, w_scales, b, g, out):
+    nc = tc.nc
+    x2 = x[0]
+    out2 = out[0].rearrange("s h d -> s (h d)")
+
+    with ExitStack() as ctx:
+        keep = ctx.enter_context(tc.tile_pool(name="keep", bufs=1))
+        work = ctx.enter_context(tc.tile_pool(name="work", bufs=3))
+        psum = ctx.enter_context(tc.psum_pool(name="psum", bufs=1))
+        ctx.enter_context(tc.manual_schedule())
+
+        vec = keep.tile([P, C // 2], BF16, name="vec")
+        ident = keep.tile([P, P], F32, name="ident")
+        pick = keep.tile([P, 4], BF16, name="pick")
+        bias = keep.tile([P, C], BF16, name="bias")
+        rot = keep.tile([P, TILES, 256], BF16, name="rot")
+        tab_sb = keep.tile([P, TILES, 2, P], F32, name="tab_sb")
+        planes = [
+            keep.tile([P, PASSES, NCOL * (c1 - c0)], U8, name="plane%d" % c0, align_bytes=64) for c0, c1 in LOADS
+        ]
+        words0 = [keep.tile([P, 2, 2 * NCOL], U8, name="words0_%d" % j, align_bytes=64) for j in range(THIRDS)]
+        words = [
+            keep.tile([P, PASSES, 2 * NCOL * (c1 - c0)], U8, name="words%d" % c0, align_bytes=64)
+            for c0, c1 in LOADS[1:]
+        ]
+        x_first = [keep.tile([P, 1024], BF16, name="x0_%d" % j) for j in range(THIRDS)]
+        x_rest = [keep.tile([P, C], BF16, name="x%d" % t) for t in range(1, TILES)]
+        codes = [
+            [keep.tile([P, 256], U32, name="codes%d_%d" % (t, j), align_bytes=64) for j in range(THIRDS)]
+            for t in range(TILES)
+        ]
+        xscale = [
+            [keep.tile([P, 256], U8, name="xscale%d_%d" % (t, j), align_bytes=64) for j in range(THIRDS)]
+            for t in range(TILES)
+        ]
+
+        def load_scales(i):
+            c0, c1 = LOADS[i]
+            for r in range(4):
+                nc.sync.dma_start(
+                    out=planes[i][r:P:32, :, :].bitcast(I32),
+                    in_=w_scales[:, r:16:4, NCOL * c0 : NCOL * c1].rearrange("g q n -> q g n").bitcast(I32),
+                )
+
+        def load_words(dst, g0, g1, c0, c1):
+            nc.sync.dma_start(
+                out=dst[:].bitcast(I32),
+                in_=w_words[g0:g1, :, 2 * NCOL * c0 : 2 * NCOL * c1].rearrange("g p n -> p g n").bitcast(I32),
+            )
+
+        nc.vector.memset(vec[:].bitcast(I32), 0)
+        nc.vector.memset(planes[0][:].bitcast(I32), 0)
+        nc.vector.memset(planes[1][:].bitcast(I32), 0)
+        make_identity(nc, ident[:])
+        nc.gpsimd.memset(planes[2][:].bitcast(I32), 0)
+        nc.gpsimd.memset(planes[3][:].bitcast(I32), 0)
+        nc.vector.tensor_copy(out=pick[:], in_=ident[:, 0:4])
+
+        nc.scalar.dma_start(out=vec[0:2, :], in_=b.rearrange("(r n) -> r n", r=2))
+        nc.scalar.dma_start(out=vec[2:3, 0:HD], in_=g.rearrange("(r n) -> r n", r=1))
+        for j in range(THIRDS):
+            nc.sync.dma_start(out=x_first[j][:], in_=x2[0:P, 1024 * j : 1024 * (j + 1)])
+        nc.sync.dma_start(out=rot[:], in_=freqs[0].rearrange("(t p) o j i k -> p t (o j i k)", p=P))
+        load_scales(0)
+        for j in range(THIRDS):
+            load_words(words0[j], 2 * j, 2 * j + 2, 0, 1)
+        nc.sync.dma_start(out=x_rest[0][:], in_=x2[P : 2 * P, :])
+        for i in range(1, len(LOADS)):
+            load_scales(i)
+            load_words(words[i - 1], 0, PASSES, LOADS[i][0], LOADS[i][1])
+            if i >= 2:
+                nc.sync.dma_start(out=x_rest[i - 1][:], in_=x2[P * i : P * (i + 1), :])
+
+        g_ps = psum.tile([P, HD], F32, name="g_ps", tag="tab1", bufs=1)
+        nc.tensor.matmul(g_ps[:], lhsT=pick[:, 2:3].to_broadcast([P, P]), rhs=vec[:, 0:HD], start=True, stop=True)
+        for j in range(3):
+            b_ps = psum.tile([P, 2 * NCOL], BF16, name="b_ps", tag="acc", bufs=3)
+            for h in range(2):
+                c = 2 * j + h
+                nc.tensor.matmul(
+                    b_ps[:, NCOL * h : NCOL * (h + 1)],
+                    lhsT=pick[:, c // 3 : c // 3 + 1].to_broadcast([P, P]),
+                    rhs=vec[:, NCOL * (c % 3) : NCOL * (c % 3 + 1)],
+                    start=True,
+                    stop=True,
+                )
+            nc.scalar.copy(out=bias[:, 1024 * j : 1024 * (j + 1)], in_=b_ps[:])
+
+        for k in range(2):
+            nc.vector.tensor_tensor(
+                out=tab_sb[:, :, k, :].rearrange("p t (j i) -> p t j i", i=2),
+                in0=rot[:].rearrange("p t (j i k) -> p t j i k", i=2, k=2)[:, :, :, :, k],
+                in1=g_ps[:].rearrange("p (j k) -> p j k", k=2)[:, :, k : k + 1]
+                .unsqueeze(1)
+                .to_broadcast([P, TILES, 64, 2]),
+                op=ALU.mult,
+            )
+
+        def x_words(t, j):
+            if t == 0:
+                return x_first[j][:].bitcast(F32)
+            return x_rest[t - 1][:, 1024 * j : 1024 * (j + 1)].bitcast(F32)
+
+        def turn(t):
+            staged = []
+            for j in range(THIRDS):
+                bank = psum.tile([P, 4, P], F32, name="bank", tag="turn", bufs=3)
+                xw = x_words(t, j)
+                for gl in range(2):
+                    for u in range(2):
+                        nc.tensor.transpose(bank[:, 2 * gl + u, :], xw[:, 256 * gl + u : 256 * (gl + 1) : 2], ident[:])
+                grouped = work.tile([P, 1024], BF16, name="grouped", align_bytes=64)
+                nc.scalar.copy(
+                    out=grouped[:].bitcast(F32).rearrange("p (g r u) -> p g r u", g=2, u=2),
+                    in_=bank[:].rearrange("p (g u) r -> p g r u", u=2),
+                )
+                staged.append(grouped)
+            return staged
+
+        def quantise(t, staged):
+            for j in range(THIRDS):
+                nc.vector.quantize_mx(out=codes[t][j][:].bitcast(E5M2), scales=xscale[t][j][:], in_=staged[j][:])
+
+        def table(half):
+            tab = psum.tile([P, 2, 2, P], F32, name="tab", tag="tab%d" % half, bufs=1)
+            nc.tensor.matmul(
+                tab[:].rearrange("p t k n -> p (t k n)"),
+                lhsT=ident[:],
+                rhs=tab_sb[:, 2 * half : 2 * half + 2, :, :].rearrange("p t k n -> p (t k n)"),
+                start=True,
+                stop=True,
+            )
+            return tab
+
+        def product(n):
+            t, c = ORDER[n]
+            i = [c0 <= c < c1 for c0, c1 in LOADS].index(True)
+            cl = c - LOADS[i][0]
+            acc = psum.tile([P, NCOL], F32, name="acc", tag="acc", bufs=3)
+            for ps in range(PASSES):
+                j, gl = divmod(ps, 2)
+                if i == 0:
+                    w = words0[j][:, gl, :]
+                else:
+                    w = words[i - 1][:, ps, 2 * NCOL * cl : 2 * NCOL * (cl + 1)]
+                nc.tensor.matmul_mx(
+                    out=acc[:],
+                    lhsT=codes[t][j][:, P * gl : P * (gl + 1)].bitcast(E5M2),
+                    lhsT_scale=xscale[t][j][:, P * gl : P * (gl + 1)],
+                    rhs=w.bitcast(E2M1),
+                    rhs_scale=planes[i][:, ps, NCOL * cl : NCOL * (cl + 1)],
+                    start=(ps == 0),
+                    stop=(ps == PASSES - 1),
+                )
+            return acc
+
+        def add_bias(n, acc):
+            c = ORDER[n][1]
+            u = work.tile([P, NCOL], F32, name="u", bufs=4)
+            nc.vector.tensor_tensor(out=u[:], in0=acc[:], in1=bias[:, NCOL * c : NCOL * (c + 1)], op=ALU.add)
+            return u
+
+        def term(n, u, k):
+            t = ORDER[n][0]
+            part = work.tile([P, NCOL], F32, name="part%d" % k)
+            nc.vector.tensor_tensor(
+                out=part[:].rearrange("p (h j i) -> p h j i", h=HEADS, i=2),
+                in0=u[:].rearrange("p (h j k) -> p h j k", h=HEADS, k=2)[:, :, :, k : k + 1].to_broadcast(
+                    [P, HEADS, 64, 2]
+                ),
+                in1=tabs[t // 2][:, t % 2, k, :]
+                .rearrange("p (j i) -> p j i", i=2)
+                .unsqueeze(1)
+                .to_broadcast([P, HEADS, 64, 2]),
+                op=ALU.mult,
+            )
+            return part
+
+        def squares(u):
+            ssq = work.tile([P, HEADS], F32, name="ssq")
+            unread = work.tile([P, NCOL], BF16, name="unread", bufs=2)
+            for h in range(HEADS):
+                cols = slice(HD * h, HD * (h + 1))
+                nc.scalar.activation(
+                    out=unread[:, cols], in_=u[:, cols], func=ACT.Square, accum_out=ssq[:, h : h + 1]
+                )
+            return ssq
+
+        def inverse_rms(ssq):
+            r = work.tile([P, HEADS], F32, name="r", bufs=4)
+            nc.scalar.activation(out=r[:], in_=ssq[:], func=ACT.Abs_reciprocal_sqrt, bias=EPS, scale=1.0 / HD)
+            return r
+
+        def join(p0, p1):
+            both = work.tile([P, NCOL], F32, name="both")
+            nc.gpsimd.tensor_tensor(out=both[:], in0=p0[:], in1=p1[:], op=ALU.add)
+            return both
+
+        def finish(n, both, r):
+            t, c = ORDER[n]
+            res = work.tile([P, NCOL], F32, name="res", bufs=8)
+            for h in range(HEADS):
+                cols = slice(HD * h, HD * (h + 1))
+                nc.scalar.activation(out=res[:, cols], in_=both[:, cols], func=ACT.Copy, scale=r[:, h : h + 1])
+            nc.sync.dma_start(out=out2[P * t : P * (t + 1), NCOL * c : NCOL * (c + 1)], in_=res[:])
+
+        def finish_last(n, u, p1, r):
+            t, c = ORDER[n]
+            p0 = work.tile([P, NCOL], F32, name="part0")
+            for h in range(HEADS):
+                cols = slice(HD * h, HD * (h + 1))
+                nc.vector.scalar_tensor_tensor(
+                    out=p0[:, cols].rearrange("p (j i) -> p j i", i=2),
+                    in0=u[:, cols].rearrange("p (j k) -> p j k", k=2)[:, :, 0:1].to_broadcast([P, 64, 2]),
+                    scalar=r[:, h : h + 1],
+                    in1=tabs[t // 2][:, t % 2, 0, :].rearrange("p (j i) -> p j i", i=2),
+                    op0=ALU.mult,
+                    op1=ALU.mult,
+                )
+            for half in range(2):
+                res = work.tile([P, NCOL // 2], F32, name="res_last", bufs=2)
+                for hl in range(2):
+                    h = 2 * half + hl
+                    cols = slice(HD * h, HD * (h + 1))
+                    nc.vector.scalar_tensor_tensor(
+                        out=res[:, HD * hl : HD * (hl + 1)],
+                        in0=p1[:, cols],
+                        scalar=r[:, h : h + 1],
+                        in1=p0[:, cols],
+                        op0=ALU.mult,
+                        op1=ALU.add,
+                    )
+                c0 = NCOL * c + 256 * half
+                nc.sync.dma_start(out=out2[P * t : P * (t + 1), c0 : c0 + 256], in_=res[:])
+
+        groups = len(ORDER)
+        last = groups - 1
+        first_use = {t: [o[0] for o in ORDER].index(t) for t in range(TILES)}
+        tabs = []
+        quantise(0, turn(0))
+        tabs.append(table(0))
+        us, rs, p0s, boths = {}, {}, {}, {}
+        for n in range(groups):
+            acc = product(n)
+            nxt = [t for t in range(1, TILES) if first_use[t] == n + 1]
+            staged = [turn(t) for t in nxt]
+            if n == 2:
+                tabs.append(table(1))
+            us[n] = add_bias(n, acc)
+            if nxt:
+                p0s[n] = term(n, us[n], 0)
+            for t, st in zip(nxt, staged):
+                quantise(t, st)
+            if n >= 1:
+                p1 = term(n - 1, us[n - 1], 1)
+                boths[n - 1] = join(p0s[n - 1], p1)
+            if n < last and not nxt:
+                p0s[n] = term(n, us[n], 0)
+            ssq = squares(us[n])
+            if 2 <= n < last:
+                finish(n - 2, boths[n - 2], rs[n - 2])
+            rs[n] = inverse_rms(ssq)
+        finish(last - 2, boths[last - 2], rs[last - 2])
+        p1 = term(last, us[last], 1)
+        finish(last - 1, boths[last - 1], rs[last - 1])
+        finish_last(last, us[last], p1, rs[last])

@@ -24,20 +24,22 @@ NCOL = 512
 CHUNKS = C // NCOL
 HEADS = NCOL // HD
 THIRDS = PASSES // 2
-LOADS = ((0, 1), (1, 2), (2, 3), (3, 6))
+PLANES = 3
+B_ROWS = 8
+B_COLS = C // B_ROWS
 ORDER = (
-    [(t, c) for c in range(3) for t in range(2)]
-    + [(2, c) for c in range(3)]
-    + [(t, c) for c in range(3, 5) for t in range(3)]
-    + [(3, c) for c in range(5)]
-    + [(t, 5) for t in range(4)]
+    [(t, c) for c in range(2) for t in range(3)]
+    + [(3, c) for c in range(2)]
+    + [(t, c) for c in range(2, CHUNKS) for t in range(TILES)]
 )
+LOAD_AFTER = {5: 3, 9: 4, 13: 5}
 
 
 def tile_selfattention_pa_kernel(tc, x, freqs, w_words, w_scales, b, g, out):
     nc = tc.nc
     x2 = x[0]
     out2 = out[0].rearrange("s h d -> s (h d)")
+    freqs2 = freqs[0].rearrange("(t p) o j i k -> p t (o j i k)", p=P)
 
     with ExitStack() as ctx:
         keep = ctx.enter_context(tc.tile_pool(name="keep", bufs=1))
@@ -45,20 +47,15 @@ def tile_selfattention_pa_kernel(tc, x, freqs, w_words, w_scales, b, g, out):
         psum = ctx.enter_context(tc.psum_pool(name="psum", bufs=1))
         ctx.enter_context(tc.manual_schedule())
 
-        vec = keep.tile([P, C // 2], BF16, name="vec")
+        vec = keep.tile([P, B_COLS], BF16, name="vec")
         ident = keep.tile([P, P], F32, name="ident")
-        pick = keep.tile([P, 4], BF16, name="pick")
+        ident_bf = keep.tile([P, P], BF16, name="ident_bf")
+        gain = keep.tile([P, HD], BF16, name="gain")
         bias = keep.tile([P, C], BF16, name="bias")
-        rot = keep.tile([P, TILES, 256], BF16, name="rot")
-        tab_sb = keep.tile([P, TILES, 2, P], F32, name="tab_sb")
-        planes = [
-            keep.tile([P, PASSES, NCOL * (c1 - c0)], U8, name="plane%d" % c0, align_bytes=64) for c0, c1 in LOADS
-        ]
+        rot = [keep.tile([P, 2, 256], BF16, name="rot%d" % h) for h in range(2)]
+        planes = [keep.tile([P, PASSES, NCOL], U8, name="plane%d" % c, align_bytes=64) for c in range(PLANES)]
         words0 = [keep.tile([P, 2, 2 * NCOL], U8, name="words0_%d" % j, align_bytes=64) for j in range(THIRDS)]
-        words = [
-            keep.tile([P, PASSES, 2 * NCOL * (c1 - c0)], U8, name="words%d" % c0, align_bytes=64)
-            for c0, c1 in LOADS[1:]
-        ]
+        words = [keep.tile([P, PASSES, 2 * NCOL], U8, name="words%d" % c, align_bytes=64) for c in range(1, CHUNKS)]
         x_first = [keep.tile([P, 1024], BF16, name="x0_%d" % j) for j in range(THIRDS)]
         x_rest = [keep.tile([P, C], BF16, name="x%d" % t) for t in range(1, TILES)]
         codes = [
@@ -70,67 +67,93 @@ def tile_selfattention_pa_kernel(tc, x, freqs, w_words, w_scales, b, g, out):
             for t in range(TILES)
         ]
 
-        def load_scales(i):
-            c0, c1 = LOADS[i]
+        def load_scales(c):
             for r in range(4):
                 nc.sync.dma_start(
-                    out=planes[i][r:P:32, :, :].bitcast(I32),
-                    in_=w_scales[:, r:16:4, NCOL * c0 : NCOL * c1].rearrange("g q n -> q g n").bitcast(I32),
+                    out=planes[c % PLANES][r:P:32, :, :].bitcast(I32),
+                    in_=w_scales[:, r:16:4, NCOL * c : NCOL * (c + 1)].rearrange("g q n -> q g n").bitcast(I32),
                 )
 
-        def load_words(dst, g0, g1, c0, c1):
+        def load_words(dst, g0, g1, c):
             nc.sync.dma_start(
                 out=dst[:].bitcast(I32),
-                in_=w_words[g0:g1, :, 2 * NCOL * c0 : 2 * NCOL * c1].rearrange("g p n -> p g n").bitcast(I32),
+                in_=w_words[g0:g1, :, 2 * NCOL * c : 2 * NCOL * (c + 1)].rearrange("g p n -> p g n").bitcast(I32),
             )
+
+        def load_chunk(c):
+            load_scales(c)
+            load_words(words[c - 1], 0, PASSES, c)
+
+        def load_x(t):
+            nc.sync.dma_start(out=x_rest[t - 1][:], in_=x2[P * t : P * (t + 1), :])
+
+        def fill_plane(c):
+            nc.vector.memset(planes[c][:].bitcast(I32), 0)
 
         nc.vector.memset(vec[:].bitcast(I32), 0)
-        nc.vector.memset(planes[0][:].bitcast(I32), 0)
-        nc.vector.memset(planes[1][:].bitcast(I32), 0)
+        fill_plane(0)
         make_identity(nc, ident[:])
-        nc.gpsimd.memset(planes[2][:].bitcast(I32), 0)
-        nc.gpsimd.memset(planes[3][:].bitcast(I32), 0)
-        nc.vector.tensor_copy(out=pick[:], in_=ident[:, 0:4])
+        nc.vector.tensor_copy(out=ident_bf[:], in_=ident[:])
+        fill_plane(1)
+        fill_plane(2)
 
-        nc.scalar.dma_start(out=vec[0:2, :], in_=b.rearrange("(r n) -> r n", r=2))
-        nc.scalar.dma_start(out=vec[2:3, 0:HD], in_=g.rearrange("(r n) -> r n", r=1))
+        nc.scalar.dma_start(out=vec[0:B_ROWS, :], in_=b.rearrange("(r n) -> r n", r=B_ROWS))
+        nc.scalar.dma_start(out=vec[B_ROWS : B_ROWS + 1, 0:HD], in_=g.rearrange("(r n) -> r n", r=1))
+        nc.sync.dma_start(out=rot[0][:], in_=freqs2[:, 0:2, :])
         for j in range(THIRDS):
             nc.sync.dma_start(out=x_first[j][:], in_=x2[0:P, 1024 * j : 1024 * (j + 1)])
-        nc.sync.dma_start(out=rot[:], in_=freqs[0].rearrange("(t p) o j i k -> p t (o j i k)", p=P))
         load_scales(0)
         for j in range(THIRDS):
-            load_words(words0[j], 2 * j, 2 * j + 2, 0, 1)
-        nc.sync.dma_start(out=x_rest[0][:], in_=x2[P : 2 * P, :])
-        for i in range(1, len(LOADS)):
-            load_scales(i)
-            load_words(words[i - 1], 0, PASSES, LOADS[i][0], LOADS[i][1])
-            if i >= 2:
-                nc.sync.dma_start(out=x_rest[i - 1][:], in_=x2[P * i : P * (i + 1), :])
+            load_words(words0[j], 2 * j, 2 * j + 2, 0)
+        load_x(1)
+        nc.sync.dma_start(out=rot[1][:], in_=freqs2[:, 2:4, :])
+        load_x(2)
+        load_chunk(1)
+        load_x(3)
+        load_chunk(2)
 
-        g_ps = psum.tile([P, HD], F32, name="g_ps", tag="tab1", bufs=1)
-        nc.tensor.matmul(g_ps[:], lhsT=pick[:, 2:3].to_broadcast([P, P]), rhs=vec[:, 0:HD], start=True, stop=True)
-        for j in range(3):
-            b_ps = psum.tile([P, 2 * NCOL], BF16, name="b_ps", tag="acc", bufs=3)
-            for h in range(2):
-                c = 2 * j + h
-                nc.tensor.matmul(
-                    b_ps[:, NCOL * h : NCOL * (h + 1)],
-                    lhsT=pick[:, c // 3 : c // 3 + 1].to_broadcast([P, P]),
-                    rhs=vec[:, NCOL * (c % 3) : NCOL * (c % 3 + 1)],
-                    start=True,
-                    stop=True,
-                )
-            nc.scalar.copy(out=bias[:, 1024 * j : 1024 * (j + 1)], in_=b_ps[:])
-
-        for k in range(2):
-            nc.vector.tensor_tensor(
-                out=tab_sb[:, :, k, :].rearrange("p t (j i) -> p t j i", i=2),
-                in0=rot[:].rearrange("p t (j i k) -> p t j i k", i=2, k=2)[:, :, :, :, k],
-                in1=g_ps[:].rearrange("p (j k) -> p j k", k=2)[:, :, k : k + 1]
-                .unsqueeze(1)
-                .to_broadcast([P, TILES, 64, 2]),
-                op=ALU.mult,
+        def spread(dst, row, width):
+            nc.tensor.matmul(
+                dst, lhsT=ident_bf[:, row : row + 1].to_broadcast([P, P]), rhs=vec[:, 0:width], start=True, stop=True
             )
+
+        g_ps = psum.tile([P, HD], BF16, name="g_ps", tag="tab1", bufs=1)
+        spread(g_ps[:], B_ROWS, HD)
+        nc.scalar.copy(out=gain[:], in_=g_ps[:])
+        for j in range(B_ROWS // 2):
+            b_ps = psum.tile([P, 2 * B_COLS], BF16, name="b_ps", tag="acc", bufs=3)
+            for h in range(2):
+                spread(b_ps[:, B_COLS * h : B_COLS * (h + 1)], 2 * j + h, B_COLS)
+            nc.scalar.copy(out=bias[:, 2 * B_COLS * j : 2 * B_COLS * (j + 1)], in_=b_ps[:])
+
+        def table_parts(half):
+            full = work.tile([P, 2, 2, HD], F32, name="full", bufs=2)
+            high = work.tile([P, NCOL], BF16, name="high", bufs=2)
+            low = work.tile([P, NCOL], BF16, name="low", bufs=2)
+            quad = rot[half][:].rearrange("p t (j e) -> p t j e", e=4)
+            for k, entries in enumerate((slice(0, 4, 3), slice(2, 0, -1))):
+                nc.vector.tensor_tensor(
+                    out=full[:, :, k, :].rearrange("p t (j i) -> p t j i", i=2),
+                    in0=quad[:, :, :, entries],
+                    in1=gain[:].rearrange("p (j k) -> p j k", k=2).unsqueeze(1).to_broadcast([P, 2, 64, 2]),
+                    op=ALU.mult,
+                )
+            flat = full[:].rearrange("p t k n -> p (t k n)")
+            nc.vector.tensor_copy(out=high[:], in_=flat)
+            nc.vector.tensor_tensor(out=low[:], in0=flat, in1=high[:], op=ALU.subtract)
+            return high, low
+
+        def table(half, parts):
+            tab = psum.tile([P, 2, 2, HD], F32, name="tab", tag="tab%d" % half, bufs=1)
+            for i, part in enumerate(parts):
+                nc.tensor.matmul(
+                    tab[:].rearrange("p t k n -> p (t k n)"),
+                    lhsT=ident_bf[:],
+                    rhs=part[:],
+                    start=(i == 0),
+                    stop=(i == 1),
+                )
+            return tab
 
         def x_words(t, j):
             if t == 0:
@@ -157,34 +180,18 @@ def tile_selfattention_pa_kernel(tc, x, freqs, w_words, w_scales, b, g, out):
             for j in range(THIRDS):
                 nc.vector.quantize_mx(out=codes[t][j][:].bitcast(E5M2), scales=xscale[t][j][:], in_=staged[j][:])
 
-        def table(half):
-            tab = psum.tile([P, 2, 2, P], F32, name="tab", tag="tab%d" % half, bufs=1)
-            nc.tensor.matmul(
-                tab[:].rearrange("p t k n -> p (t k n)"),
-                lhsT=ident[:],
-                rhs=tab_sb[:, 2 * half : 2 * half + 2, :, :].rearrange("p t k n -> p (t k n)"),
-                start=True,
-                stop=True,
-            )
-            return tab
-
         def product(n):
             t, c = ORDER[n]
-            i = [c0 <= c < c1 for c0, c1 in LOADS].index(True)
-            cl = c - LOADS[i][0]
             acc = psum.tile([P, NCOL], F32, name="acc", tag="acc", bufs=3)
             for ps in range(PASSES):
                 j, gl = divmod(ps, 2)
-                if i == 0:
-                    w = words0[j][:, gl, :]
-                else:
-                    w = words[i - 1][:, ps, 2 * NCOL * cl : 2 * NCOL * (cl + 1)]
+                w = words0[j][:, gl, :] if c == 0 else words[c - 1][:, ps, :]
                 nc.tensor.matmul_mx(
                     out=acc[:],
                     lhsT=codes[t][j][:, P * gl : P * (gl + 1)].bitcast(E5M2),
                     lhsT_scale=xscale[t][j][:, P * gl : P * (gl + 1)],
                     rhs=w.bitcast(E2M1),
-                    rhs_scale=planes[i][:, ps, NCOL * cl : NCOL * (cl + 1)],
+                    rhs_scale=planes[c % PLANES][:, ps, :],
                     start=(ps == 0),
                     stop=(ps == PASSES - 1),
                 )
@@ -200,14 +207,9 @@ def tile_selfattention_pa_kernel(tc, x, freqs, w_words, w_scales, b, g, out):
             t = ORDER[n][0]
             part = work.tile([P, NCOL], F32, name="part%d" % k)
             nc.vector.tensor_tensor(
-                out=part[:].rearrange("p (h j i) -> p h j i", h=HEADS, i=2),
-                in0=u[:].rearrange("p (h j k) -> p h j k", h=HEADS, k=2)[:, :, :, k : k + 1].to_broadcast(
-                    [P, HEADS, 64, 2]
-                ),
-                in1=tabs[t // 2][:, t % 2, k, :]
-                .rearrange("p (j i) -> p j i", i=2)
-                .unsqueeze(1)
-                .to_broadcast([P, HEADS, 64, 2]),
+                out=part[:].rearrange("p (h d) -> p h d", h=HEADS),
+                in0=u[:].rearrange("p (h d) -> p h d", h=HEADS),
+                in1=tabs[t // 2][:, t % 2, k, :].unsqueeze(1).to_broadcast([P, HEADS, HD]),
                 op=ALU.mult,
             )
             return part
@@ -227,9 +229,12 @@ def tile_selfattention_pa_kernel(tc, x, freqs, w_words, w_scales, b, g, out):
             nc.scalar.activation(out=r[:], in_=ssq[:], func=ACT.Abs_reciprocal_sqrt, bias=EPS, scale=1.0 / HD)
             return r
 
+        def pairs(ap):
+            return ap.rearrange("p (j i) -> p j i", i=2)
+
         def join(p0, p1):
             both = work.tile([P, NCOL], F32, name="both")
-            nc.gpsimd.tensor_tensor(out=both[:], in0=p0[:], in1=p1[:], op=ALU.add)
+            nc.gpsimd.tensor_tensor(out=pairs(both[:]), in0=pairs(p0[:]), in1=pairs(p1[:])[:, :, ::-1], op=ALU.add)
             return both
 
         def finish(n, both, r):
@@ -239,6 +244,8 @@ def tile_selfattention_pa_kernel(tc, x, freqs, w_words, w_scales, b, g, out):
                 cols = slice(HD * h, HD * (h + 1))
                 nc.scalar.activation(out=res[:, cols], in_=both[:, cols], func=ACT.Copy, scale=r[:, h : h + 1])
             nc.sync.dma_start(out=out2[P * t : P * (t + 1), NCOL * c : NCOL * (c + 1)], in_=res[:])
+            if n in LOAD_AFTER:
+                load_chunk(LOAD_AFTER[n])
 
         def finish_last(n, u, p1, r):
             t, c = ORDER[n]
@@ -246,10 +253,10 @@ def tile_selfattention_pa_kernel(tc, x, freqs, w_words, w_scales, b, g, out):
             for h in range(HEADS):
                 cols = slice(HD * h, HD * (h + 1))
                 nc.vector.scalar_tensor_tensor(
-                    out=p0[:, cols].rearrange("p (j i) -> p j i", i=2),
-                    in0=u[:, cols].rearrange("p (j k) -> p j k", k=2)[:, :, 0:1].to_broadcast([P, 64, 2]),
+                    out=p0[:, cols],
+                    in0=u[:, cols],
                     scalar=r[:, h : h + 1],
-                    in1=tabs[t // 2][:, t % 2, 0, :].rearrange("p (j i) -> p j i", i=2),
+                    in1=tabs[t // 2][:, t % 2, 0, :],
                     op0=ALU.mult,
                     op1=ALU.mult,
                 )
@@ -259,10 +266,10 @@ def tile_selfattention_pa_kernel(tc, x, freqs, w_words, w_scales, b, g, out):
                     h = 2 * half + hl
                     cols = slice(HD * h, HD * (h + 1))
                     nc.vector.scalar_tensor_tensor(
-                        out=res[:, HD * hl : HD * (hl + 1)],
-                        in0=p1[:, cols],
+                        out=pairs(res[:, HD * hl : HD * (hl + 1)]),
+                        in0=pairs(p1[:, cols])[:, :, ::-1],
                         scalar=r[:, h : h + 1],
-                        in1=p0[:, cols],
+                        in1=pairs(p0[:, cols]),
                         op0=ALU.mult,
                         op1=ALU.add,
                     )
@@ -273,29 +280,35 @@ def tile_selfattention_pa_kernel(tc, x, freqs, w_words, w_scales, b, g, out):
         last = groups - 1
         first_use = {t: [o[0] for o in ORDER].index(t) for t in range(TILES)}
         tabs = []
+        parts = table_parts(0)
         quantise(0, turn(0))
-        tabs.append(table(0))
-        us, rs, p0s, boths = {}, {}, {}, {}
+        tabs.append(table(0, parts))
+        us, ssqs, rs, p0s, boths = {}, {}, {}, {}, {}
         for n in range(groups):
             acc = product(n)
             nxt = [t for t in range(1, TILES) if first_use[t] == n + 1]
             staged = [turn(t) for t in nxt]
-            if n == 2:
-                tabs.append(table(1))
+            if n == 1:
+                tabs.append(table(1, parts))
             us[n] = add_bias(n, acc)
             if nxt:
                 p0s[n] = term(n, us[n], 0)
             for t, st in zip(nxt, staged):
                 quantise(t, st)
+            if n == 0:
+                parts = table_parts(1)
             if n >= 1:
                 p1 = term(n - 1, us[n - 1], 1)
                 boths[n - 1] = join(p0s[n - 1], p1)
             if n < last and not nxt:
                 p0s[n] = term(n, us[n], 0)
-            ssq = squares(us[n])
+            ssqs[n] = squares(us[n])
             if 2 <= n < last:
                 finish(n - 2, boths[n - 2], rs[n - 2])
-            rs[n] = inverse_rms(ssq)
+            if n == 1:
+                rs[0] = inverse_rms(ssqs[0])
+            if n >= 1:
+                rs[n] = inverse_rms(ssqs[n])
         finish(last - 2, boths[last - 2], rs[last - 2])
         p1 = term(last, us[last], 1)
         finish(last - 1, boths[last - 1], rs[last - 1])

from contextlib import ExitStack

import concourse.mybir as mybir
from concourse.masks import make_identity

S, C, HD = 512, 3072, 128
EPS = 1e-6
FLOPS = 2 * S * C * C

F32 = mybir.dt.float32
BF16 = mybir.dt.bfloat16
I32 = mybir.dt.int32
U32 = mybir.dt.uint32
U8 = mybir.dt.uint8
E5M2 = mybir.dt.float8_e5m2_x4
E2M1 = mybir.dt.float4_e2m1fn_x4
ALU = mybir.AluOpType
ACT = mybir.ActivationFunctionType

P = 128
PASSES = C // 512
TILES = S // P
NCOL = 512
CHUNKS = C // NCOL
HEADS = NCOL // HD
THIRDS = PASSES // 2
PLANES = 3
B_ROWS = 8
B_COLS = C // B_ROWS
ORDER = (
    [(t, c) for c in range(2) for t in range(3)]
    + [(3, c) for c in range(2)]
    + [(t, c) for c in range(2, CHUNKS) for t in range(TILES)]
)
LOAD_AFTER = {5: 3, 9: 4, 13: 5}


def tile_selfattention_pa_kernel(tc, x, freqs, w_words, w_scales, b, g, out):
    nc = tc.nc
    x2 = x[0]
    out2 = out[0].rearrange("s h d -> s (h d)")
    freqs2 = freqs[0].rearrange("(t p) o j i k -> p t (o j i k)", p=P)

    with ExitStack() as ctx:
        keep = ctx.enter_context(tc.tile_pool(name="keep", bufs=1))
        work = ctx.enter_context(tc.tile_pool(name="work", bufs=3))
        psum = ctx.enter_context(tc.psum_pool(name="psum", bufs=1))
        ctx.enter_context(tc.manual_schedule())

        vec = keep.tile([P, B_COLS], BF16, name="vec")
        ident = keep.tile([P, P], F32, name="ident")
        ident_bf = keep.tile([P, P], BF16, name="ident_bf")
        gain = keep.tile([P, HD], BF16, name="gain")
        bias = keep.tile([P, C], BF16, name="bias")
        rot = [keep.tile([P, 2, 256], BF16, name="rot%d" % h) for h in range(2)]
        planes = [keep.tile([P, PASSES, NCOL], U8, name="plane%d" % c, align_bytes=64) for c in range(PLANES)]
        words0 = [keep.tile([P, 2, 2 * NCOL], U8, name="words0_%d" % j, align_bytes=64) for j in range(THIRDS)]
        words = [keep.tile([P, PASSES, 2 * NCOL], U8, name="words%d" % c, align_bytes=64) for c in range(1, CHUNKS)]
        x_first = [keep.tile([P, 1024], BF16, name="x0_%d" % j) for j in range(THIRDS)]
        x_rest = [keep.tile([P, C], BF16, name="x%d" % t) for t in range(1, TILES)]
        codes = [
            [keep.tile([P, 256], U32, name="codes%d_%d" % (t, j), align_bytes=64) for j in range(THIRDS)]
            for t in range(TILES)
        ]
        xscale = [
            [keep.tile([P, 256], U8, name="xscale%d_%d" % (t, j), align_bytes=64) for j in range(THIRDS)]
            for t in range(TILES)
        ]

        def load_scales(c):
            for r in range(4):
                nc.sync.dma_start(
                    out=planes[c % PLANES][r:P:32, :, :].bitcast(I32),
                    in_=w_scales[:, r:16:4, NCOL * c : NCOL * (c + 1)].rearrange("g q n -> q g n").bitcast(I32),
                )

        def load_words(dst, g0, g1, c):
            nc.sync.dma_start(
                out=dst[:].bitcast(I32),
                in_=w_words[g0:g1, :, 2 * NCOL * c : 2 * NCOL * (c + 1)].rearrange("g p n -> p g n").bitcast(I32),
            )

        def load_chunk(c):
            load_scales(c)
            load_words(words[c - 1], 0, PASSES, c)

        def load_x(t):
            nc.sync.dma_start(out=x_rest[t - 1][:], in_=x2[P * t : P * (t + 1), :])

        def fill_plane(c):
            nc.vector.memset(planes[c][:].bitcast(I32), 0)

        nc.vector.memset(vec[:].bitcast(I32), 0)
        fill_plane(0)
        make_identity(nc, ident[:])
        nc.vector.tensor_copy(out=ident_bf[:], in_=ident[:])
        fill_plane(1)
        fill_plane(2)

        nc.scalar.dma_start(out=vec[0:B_ROWS, :], in_=b.rearrange("(r n) -> r n", r=B_ROWS))
        nc.scalar.dma_start(out=vec[B_ROWS : B_ROWS + 1, 0:HD], in_=g.rearrange("(r n) -> r n", r=1))
        nc.sync.dma_start(out=rot[0][:], in_=freqs2[:, 0:2, :])
        for j in range(THIRDS):
            nc.sync.dma_start(out=x_first[j][:], in_=x2[0:P, 1024 * j : 1024 * (j + 1)])
        load_scales(0)
        for j in range(THIRDS):
            load_words(words0[j], 2 * j, 2 * j + 2, 0)
        load_x(1)
        nc.sync.dma_start(out=rot[1][:], in_=freqs2[:, 2:4, :])
        load_x(2)
        load_chunk(1)
        load_x(3)
        load_chunk(2)

        def spread(dst, row, width):
            nc.tensor.matmul(
                dst, lhsT=ident_bf[:, row : row + 1].to_broadcast([P, P]), rhs=vec[:, 0:width], start=True, stop=True
            )

        g_ps = psum.tile([P, HD], BF16, name="g_ps", tag="tab1", bufs=1)
        spread(g_ps[:], B_ROWS, HD)
        nc.scalar.copy(out=gain[:], in_=g_ps[:])
        for j in range(B_ROWS // 2):
            b_ps = psum.tile([P, 2 * B_COLS], BF16, name="b_ps", tag="acc", bufs=3)
            for h in range(2):
                spread(b_ps[:, B_COLS * h : B_COLS * (h + 1)], 2 * j + h, B_COLS)
            nc.scalar.copy(out=bias[:, 2 * B_COLS * j : 2 * B_COLS * (j + 1)], in_=b_ps[:])

        def table_parts(half):
            full = work.tile([P, 2, 2, HD], F32, name="full", bufs=2)
            high = work.tile([P, NCOL], BF16, name="high", bufs=2)
            low = work.tile([P, NCOL], BF16, name="low", bufs=2)
            quad = rot[half][:].rearrange("p t (j e) -> p t j e", e=4)
            for k, entries in enumerate((slice(0, 4, 3), slice(2, 0, -1))):
                nc.vector.tensor_tensor(
                    out=full[:, :, k, :].rearrange("p t (j i) -> p t j i", i=2),
                    in0=quad[:, :, :, entries],
                    in1=gain[:].rearrange("p (j k) -> p j k", k=2).unsqueeze(1).to_broadcast([P, 2, 64, 2]),
                    op=ALU.mult,
                )
            flat = full[:].rearrange("p t k n -> p (t k n)")
            nc.vector.tensor_copy(out=high[:], in_=flat)
            nc.vector.tensor_tensor(out=low[:], in0=flat, in1=high[:], op=ALU.subtract)
            return high, low

        def table(half, parts):
            tab = psum.tile([P, 2, 2, HD], F32, name="tab", tag="tab%d" % half, bufs=1)
            for i, part in enumerate(parts):
                nc.tensor.matmul(
                    tab[:].rearrange("p t k n -> p (t k n)"),
                    lhsT=ident_bf[:],
                    rhs=part[:],
                    start=(i == 0),
                    stop=(i == 1),
                )
            return tab

        def x_words(t, j):
            if t == 0:
                return x_first[j][:].bitcast(F32)
            return x_rest[t - 1][:, 1024 * j : 1024 * (j + 1)].bitcast(F32)

        def turn(t):
            staged = []
            for j in range(THIRDS):
                bank = psum.tile([P, 4, P], F32, name="bank", tag="turn", bufs=3)
                xw = x_words(t, j)
                for gl in range(2):
                    for u in range(2):
                        nc.tensor.transpose(bank[:, 2 * gl + u, :], xw[:, 256 * gl + u : 256 * (gl + 1) : 2], ident[:])
                grouped = work.tile([P, 1024], BF16, name="grouped", align_bytes=64)
                nc.scalar.copy(
                    out=grouped[:].bitcast(F32).rearrange("p (g r u) -> p g r u", g=2, u=2),
                    in_=bank[:].rearrange("p (g u) r -> p g r u", u=2),
                )
                staged.append(grouped)
            return staged

        def quantise(t, staged):
            for j in range(THIRDS):
                nc.vector.quantize_mx(out=codes[t][j][:].bitcast(E5M2), scales=xscale[t][j][:], in_=staged[j][:])

        def product(n):
            t, c = ORDER[n]
            acc = psum.tile([P, NCOL], F32, name="acc", tag="acc", bufs=3)
            for ps in range(PASSES):
                j, gl = divmod(ps, 2)
                w = words0[j][:, gl, :] if c == 0 else words[c - 1][:, ps, :]
                nc.tensor.matmul_mx(
                    out=acc[:],
                    lhsT=codes[t][j][:, P * gl : P * (gl + 1)].bitcast(E5M2),
                    lhsT_scale=xscale[t][j][:, P * gl : P * (gl + 1)],
                    rhs=w.bitcast(E2M1),
                    rhs_scale=planes[c % PLANES][:, ps, :],
                    start=(ps == 0),
                    stop=(ps == PASSES - 1),
                )
            return acc

        def add_bias(n, acc):
            c = ORDER[n][1]
            u = work.tile([P, NCOL], F32, name="u", bufs=4)
            nc.vector.tensor_tensor(out=u[:], in0=acc[:], in1=bias[:, NCOL * c : NCOL * (c + 1)], op=ALU.add)
            return u

        def term(n, u, k):
            t = ORDER[n][0]
            part = work.tile([P, NCOL], F32, name="part%d" % k)
            nc.vector.tensor_tensor(
                out=part[:].rearrange("p (h d) -> p h d", h=HEADS),
                in0=u[:].rearrange("p (h d) -> p h d", h=HEADS),
                in1=tabs[t // 2][:, t % 2, k, :].unsqueeze(1).to_broadcast([P, HEADS, HD]),
                op=ALU.mult,
            )
            return part

        def squares(u):
            ssq = work.tile([P, HEADS], F32, name="ssq")
            unread = work.tile([P, NCOL], BF16, name="unread", bufs=2)
            for h in range(HEADS):
                cols = slice(HD * h, HD * (h + 1))
                nc.scalar.activation(
                    out=unread[:, cols], in_=u[:, cols], func=ACT.Square, accum_out=ssq[:, h : h + 1]
                )
            return ssq

        def inverse_rms(ssq):
            r = work.tile([P, HEADS], F32, name="r", bufs=4)
            nc.scalar.activation(out=r[:], in_=ssq[:], func=ACT.Abs_reciprocal_sqrt, bias=EPS, scale=1.0 / HD)
            return r

        def pairs(ap):
            return ap.rearrange("p (j i) -> p j i", i=2)

        def join(p0, p1):
            both = work.tile([P, NCOL], F32, name="both")
            nc.gpsimd.tensor_tensor(out=pairs(both[:]), in0=pairs(p0[:]), in1=pairs(p1[:])[:, :, ::-1], op=ALU.add)
            return both

        def finish(n, both, r):
            t, c = ORDER[n]
            res = work.tile([P, NCOL], F32, name="res", bufs=8)
            for h in range(HEADS):
                cols = slice(HD * h, HD * (h + 1))
                nc.scalar.activation(out=res[:, cols], in_=both[:, cols], func=ACT.Copy, scale=r[:, h : h + 1])
            nc.sync.dma_start(out=out2[P * t : P * (t + 1), NCOL * c : NCOL * (c + 1)], in_=res[:])
            if n in LOAD_AFTER:
                load_chunk(LOAD_AFTER[n])

        def finish_last(n, u, p1, r):
            t, c = ORDER[n]
            p0 = work.tile([P, NCOL], F32, name="part0")
            for h in range(HEADS):
                cols = slice(HD * h, HD * (h + 1))
                nc.vector.scalar_tensor_tensor(
                    out=p0[:, cols],
                    in0=u[:, cols],
                    scalar=r[:, h : h + 1],
                    in1=tabs[t // 2][:, t % 2, 0, :],
                    op0=ALU.mult,
                    op1=ALU.mult,
                )
            for half in range(2):
                res = work.tile([P, NCOL // 2], F32, name="res_last", bufs=2)
                for hl in range(2):
                    h = 2 * half + hl
                    cols = slice(HD * h, HD * (h + 1))
                    nc.vector.scalar_tensor_tensor(
                        out=pairs(res[:, HD * hl : HD * (hl + 1)]),
                        in0=pairs(p1[:, cols])[:, :, ::-1],
                        scalar=r[:, h : h + 1],
                        in1=pairs(p0[:, cols]),
                        op0=ALU.mult,
                        op1=ALU.add,
                    )
                c0 = NCOL * c + 256 * half
                nc.sync.dma_start(out=out2[P * t : P * (t + 1), c0 : c0 + 256], in_=res[:])

        groups = len(ORDER)
        last = groups - 1
        first_use = {t: [o[0] for o in ORDER].index(t) for t in range(TILES)}
        tabs = []
        parts = table_parts(0)
        quantise(0, turn(0))
        tabs.append(table(0, parts))
        us, ssqs, rs, p0s, boths = {}, {}, {}, {}, {}
        for n in range(groups):
            acc = product(n)
            nxt = [t for t in range(1, TILES) if first_use[t] == n + 1]
            staged = [turn(t) for t in nxt]
            if n == 1:
                tabs.append(table(1, parts))
            us[n] = add_bias(n, acc)
            if nxt:
                p0s[n] = term(n, us[n], 0)
            for t, st in zip(nxt, staged):
                quantise(t, st)
            if n == 0:
                parts = table_parts(1)
            if n >= 1:
                p1 = term(n - 1, us[n - 1], 1)
                boths[n - 1] = join(p0s[n - 1], p1)
            if n < last and not nxt:
                p0s[n] = term(n, us[n], 0)
            ssqs[n] = squares(us[n])
            if 2 <= n < last:
                finish(n - 2, boths[n - 2], rs[n - 2])
            if n == 1:
                rs[0] = inverse_rms(ssqs[0])
            if n >= 1:
                rs[n] = inverse_rms(ssqs[n])
        finish(last - 2, boths[last - 2], rs[last - 2])
        p1 = term(last, us[last], 1)
        finish(last - 1, boths[last - 1], rs[last - 1])
        finish_last(last, us[last], p1, rs[last])
